import numpy as np
import ml_dtypes


def mxq(x, axis, fmt="e4m3"):
    dtype, down = {"e4m3": (ml_dtypes.float8_e4m3fn, 7), "e5m2": (ml_dtypes.float8_e5m2, 14)}[fmt]
    v = np.moveaxis(np.asarray(x, np.float32).astype(ml_dtypes.bfloat16).astype(np.float64), axis, -1)
    blocks = v.reshape(v.shape[:-1] + (-1, 32))
    amax = np.abs(blocks).max(-1, keepdims=True)
    byte = np.maximum(np.where(amax > 0, np.frexp(amax)[1] - 1 + 127, 0) - down, 1)
    scale = np.exp2(byte - 127.0)
    codes = (blocks / scale).astype(np.float32).astype(dtype).astype(np.float64)
    return np.moveaxis((codes * scale).reshape(v.shape), -1, axis)


WIDE = False


def mx_kscale(k):
    if not WIDE:
        return np.ones(k)
    levels = np.array([10, -10, 5, -5, 0])
    if k % 512:
        return np.exp2(np.random.permutation(np.resize(levels, k // 32))).repeat(32)
    a = np.empty((k // 512, 16))
    for p in range(k // 512):
        a[p, :8] = np.random.permutation(np.resize(levels, 8))
        for g in range(8):
            far = levels[np.abs(levels - a[p, g]) >= 10]
            a[p, g + 8] = far[np.random.randint(len(far))]
    return np.exp2(a.ravel()).repeat(32)


BF16 = ml_dtypes.bfloat16


def bf(x):
    return np.asarray(x, np.float32).astype(BF16)


def f64(x):
    return np.asarray(x).astype(np.float64)


B, SIDE, HE, Z, HD, XO = 4096, 32, 1024, 512, 1024, 512


def setup_inputs():
    n = np.random.standard_normal
    s = mx_kscale(HD)
    return {"hd": bf(np.tanh(n((B, HD))) * s),
            "W_mu_d": bf(n((XO, HD)) * 1.5 / np.sqrt(HD) / s[None, :]),
            "b_mu_d": bf(n(XO) * 0.3),
            "W_ls_d": bf(n((XO, HD)) * 1.5 / np.sqrt(HD) / s[None, :]),
            "b_ls_d": bf(n(XO) * 0.3),
            "eps_x": bf(n((B, XO)))}


def reference(hd, W_mu_d, b_mu_d, W_ls_d, b_ls_d, eps_x):
    hq = mxq(f64(hd), 1, "e4m3")
    mu_d = (hq @ mxq(f64(W_mu_d), 1, "e4m3").T) + f64(b_mu_d)
    ls_d = (hq @ mxq(f64(W_ls_d), 1, "e4m3").T) + f64(b_ls_d)
    return mu_d + np.exp(0.5 * ls_d) * f64(eps_x)

@@ -1,0 +1,316 @@
+from contextlib import ExitStack
+
+import concourse.mybir as mybir
+from concourse.masks import make_identity
+
+F32 = mybir.dt.float32
+BF16 = mybir.dt.bfloat16
+U32 = mybir.dt.uint32
+U8 = mybir.dt.uint8
+FP8X4 = mybir.dt.float8_e4m3fn_x4
+ACT = mybir.ActivationFunctionType
+ALU = mybir.AluOpType
+
+P = 128
+B, K, XO = 4096, 1024, 512
+T4 = 4
+GROUPS = B // (P * T4)
+K_PASS = 512
+PASSES = K // K_PASS
+LAG = 2
+FLOPS = 2 * B * K * 2 * XO
+
+
+def tile_vae_pb_t_kernel(tc, hd, W_mu_d, b_mu_d, W_ls_d, b_ls_d, eps_x, out):
+    nc = tc.nc
+    hd_v = hd.rearrange("(g p i) k -> g p (i k)", p=P, i=T4)
+    hd_pieces = hd.rearrange("(g p i) k -> g i p k", p=P, i=T4)
+    eps_v = eps_x.rearrange("(g p i) n -> g p (i n)", p=P, i=T4)
+    out_v = out.rearrange("(g p i) n -> g p (i n)", p=P, i=T4)
+
+    with ExitStack() as ctx:
+        const = ctx.enter_context(tc.tile_pool(name="const", bufs=1))
+        raw = ctx.enter_context(tc.tile_pool(name="raw", bufs=4))
+        epsp = ctx.enter_context(tc.tile_pool(name="epsp", bufs=GROUPS))
+        grpp = ctx.enter_context(tc.tile_pool(name="grpp", bufs=2))
+        grpw = ctx.enter_context(tc.tile_pool(name="grpw", bufs=4))
+        hcp = ctx.enter_context(tc.tile_pool(name="hcp", bufs=5))
+        etp = ctx.enter_context(tc.tile_pool(name="etp", bufs=4))
+        prodp = ctx.enter_context(tc.tile_pool(name="prodp", bufs=4))
+        resp = ctx.enter_context(tc.tile_pool(name="resp", bufs=3))
+        psum = ctx.enter_context(tc.psum_pool(name="psum", bufs=1))
+        ctx.enter_context(tc.manual_schedule())
+
+        def bank(tag, shape, dtype=F32):
+            return psum.tile(shape, dtype, tag=tag, name="ps" + tag)
+
+        ident = const.tile([P, P], F32, name="ident")
+        make_identity(nc, ident[:])
+        ident_bf = const.tile([P, P], BF16, name="ident_bf")
+        make_identity(nc, ident_bf[:])
+        brow_mu = const.tile([P, XO], BF16, name="brow_mu")
+        nc.vector.memset(brow_mu[:], 0.0)
+        bcol = const.tile([P, P], BF16, name="bcol")
+        nc.vector.memset(bcol[:], 0.0)
+        ones = const.tile([P, P], BF16, name="ones")
+        nc.vector.memset(ones[:], 1.0)
+        warm = const.tile([P, 1], F32, name="warm")
+        nc.vector.memset(warm[:], 0.0)
+        nc.scalar.dma_start(out=bcol[0:T4, :], in_=b_ls_d.rearrange("(j q) -> j q", q=P))
+        nc.scalar.dma_start(out=brow_mu[0:1, :], in_=b_mu_d.rearrange("(o n) -> o n", o=1))
+        warm2 = const.tile([P, 1], F32, name="warm2")
+        nc.scalar.activation(out=warm2[:], in_=warm[:], func=ACT.Exp)
+
+        hd_sb, eps_sb, w_sb = {}, {}, {}
+        pend, grp, hq = {}, {}, {}
+        wpend, wls_grp, wq = {}, {}, {}
+        ls_ps, et_sb, e_ps, mu_ps, prod, res = {}, {}, {}, {}, {}, {}
+        small = {}
+
+        def load_hd(g, pieces):
+            t = raw.tile([P, T4 * K], BF16, tag="raw", name="hd_sb")
+            if pieces:
+                for i in range(T4):
+                    nc.sync.dma_start(out=t[:, i * K : (i + 1) * K], in_=hd_pieces[g, i])
+            else:
+                nc.sync.dma_start(out=t[:], in_=hd_v[g])
+            hd_sb[g] = t
+
+        def load_w(nm, w):
+            t = const.tile([P, T4 * K], BF16, name=nm)
+            for r in range(T4):
+                nc.sync.dma_start(out=t[:, r * K : (r + 1) * K], in_=w[r * P : (r + 1) * P, :])
+            w_sb[nm] = t
+
+        def load_eps(g):
+            t = epsp.tile([P, T4 * XO], BF16, tag="eps", name="eps_sb")
+            nc.sync.dma_start(out=t[:], in_=eps_v[g])
+            eps_sb[g] = t
+
+        def transpose_tile(src, i, tag):
+            words = src[:].bitcast(F32)
+            bk = bank(tag, [P, 4, P])
+            for s in range(4):
+                c0 = i * 512 + (s // 2) * 256 + s % 2
+                nc.tensor.transpose(bk[:, s, :], words[:, c0 : (c0 // 256 + 1) * 256 : 2], ident[:])
+            return bk
+
+        def copy_out(eng, dst, bk):
+            src = bk[:].rearrange("p (g u) b -> p g b u", u=2)
+            if eng == "V":
+                nc.vector.tensor_copy(out=dst, in_=src)
+            else:
+                nc.scalar.copy(out=dst, in_=src)
+
+        def group_slot(t, i):
+            gw = t[:].bitcast(F32).rearrange("p (g c u) -> p g c u", g=PASSES, u=2)
+            return gw[:, :, i * P : (i + 1) * P, :]
+
+        def quantise_group(t, pool, tag):
+            codes = pool.tile([P, PASSES * 512], U32, tag=tag + "c", name=tag + "c", align_bytes=64)
+            scales = pool.tile([P, PASSES * 512], U8, tag=tag + "s", name=tag + "s", align_bytes=64)
+            for c in range(PASSES):
+                nc.vector.quantize_mx(
+                    out=codes[:, c * 512 : (c + 1) * 512].bitcast(FP8X4),
+                    scales=scales[:, c * 512 : (c + 1) * 512],
+                    in_=t[:, c * 2048 : (c + 1) * 2048],
+                )
+            return codes, scales
+
+        def trh(g, i, tag):
+            pend[g, i] = transpose_tile(hd_sb[g], i, tag)
+
+        def cph(eng, g, i):
+            if g not in grp:
+                grp[g] = grpp.tile([P, T4 * K], BF16, tag="grp", name="grp", align_bytes=64)
+            copy_out(eng, group_slot(grp[g], i), pend[g, i])
+
+        def qh(g):
+            if g == "wmu":
+                hq[g] = quantise_group(grp[g], const, "wmu")
+            else:
+                hq[g] = quantise_group(grp[g], hcp, "h")
+
+        def trw(nm, r, tag):
+            wpend[nm, r] = transpose_tile(w_sb[nm], r, tag)
+
+        def cp_wls(r):
+            t = grpw.tile([P, K], BF16, tag="grpw", name="grpw", align_bytes=64)
+            copy_out("S", t[:].bitcast(F32).rearrange("p (g c u) -> p g c u", g=PASSES, u=2), wpend["wls", r])
+            wls_grp[r] = t
+
+        def q_wls(r):
+            codes = const.tile([P, PASSES * P], U32, name="wlsc" + str(r), align_bytes=64)
+            scales = const.tile([P, PASSES * P], U8, name="wlss" + str(r), align_bytes=64)
+            nc.vector.quantize_mx(out=codes[:].bitcast(FP8X4), scales=scales[:], in_=wls_grp[r][:])
+            wq[r] = (codes, scales)
+
+        def cp_wmu(eng, r):
+            cph(eng, "wmu", r)
+
+        def mx(acc, stat, s_pitch, s0, mov, m_pitch):
+            for c in range(PASSES):
+                a = c * s_pitch + s0
+                b = c * m_pitch
+                nc.tensor.matmul_mx(
+                    out=acc,
+                    lhsT=stat[0][:, a : a + P].bitcast(FP8X4),
+                    lhsT_scale=stat[1][:, a : a + P],
+                    rhs=mov[0][:, b : b + 512].bitcast(FP8X4),
+                    rhs_scale=mov[1][:, b : b + 512],
+                    start=(c == 0),
+                    stop=(c == PASSES - 1),
+                )
+
+        def bias_t():
+            small["bt"] = bank("B0", [P, P], BF16)
+            nc.tensor.transpose(small["bt"][:], bcol[:], ident_bf[:])
+            small["c"] = bank("B1", [P, XO])
+            nc.tensor.matmul(out=small["c"][:], lhsT=ones[:], rhs=brow_mu[:], start=True, stop=True)
+
+        half_bls = const.tile([P, T4], F32, name="half_bls")
+        c4 = const.tile([P, T4 * XO], F32, name="c4")
+
+        def bias_half():
+            nc.vector.tensor_scalar_mul(out=half_bls[:], in0=small["bt"][:, 0:T4], scalar1=0.5)
+
+        def bias_c4():
+            for i in range(T4):
+                nc.vector.tensor_copy(out=c4[:, i * XO : (i + 1) * XO], in_=small["c"][:])
+
+        def ls(g, j):
+            ls_ps[g, j] = bank("A" + str(j), [P, 512])
+            mx(ls_ps[g, j][:], wq[j], P, 0, hq[g], 512)
+
+        def ex(g, j):
+            et_sb[g, j] = etp.tile([P, 512], F32, tag="et", name="et")
+            nc.scalar.activation(
+                out=et_sb[g, j][:], in_=ls_ps[g, j][:], func=ACT.Exp, bias=half_bls[:, j : j + 1], scale=0.5
+            )
+
+        def etr(g, j):
+            e_ps[g, j] = bank("A" + str(j), [P, T4, P])
+            for i in range(T4):
+                nc.tensor.transpose(e_ps[g, j][:, i, :], et_sb[g, j][:, i * P : (i + 1) * P], ident[:])
+
+        def by_tile(t):
+            return t[:].rearrange("p (i n) -> p i n", i=T4)
+
+        def ph(g, j):
+            if g not in prod:
+                prod[g] = prodp.tile([P, T4 * XO], F32, tag="prod", name="prod")
+            cols = slice(j * P, (j + 1) * P)
+            nc.vector.tensor_tensor(
+                out=by_tile(prod[g])[:, :, cols], in0=e_ps[g, j][:], in1=by_tile(eps_sb[g])[:, :, cols], op=ALU.mult
+            )
+
+        def pc(g, j):
+            cols = slice(j * P, (j + 1) * P)
+            nc.gpsimd.tensor_tensor(
+                out=by_tile(prod[g])[:, :, cols], in0=by_tile(prod[g])[:, :, cols], in1=by_tile(c4)[:, :, cols], op=ALU.add
+            )
+
+        def mu(g, i):
+            mu_ps[g, i] = bank("B" + str(i), [P, XO])
+            mx(mu_ps[g, i][:], hq[g], 512, i * P, hq["wmu"], 512)
+
+        def rs(g, i):
+            if g not in res:
+                res[g] = resp.tile([P, T4 * XO], F32, tag="res", name="res")
+            cols = slice(i * XO, (i + 1) * XO)
+            nc.vector.tensor_tensor(out=res[g][:, cols], in0=mu_ps[g, i][:], in1=prod[g][:, cols], op=ALU.add)
+
+        def store(g, i0, i1):
+            cols = slice(i0 * XO, i1 * XO)
+            nc.sync.dma_start(out=out_v[g][:, cols], in_=res[g][:, cols])
+
+        R4 = range(T4)
+        load_hd(0, True)
+        load_w("wls", W_ls_d)
+        load_hd(1, True)
+        load_eps(0)
+        load_hd(2, False)
+        load_w("wmu", W_mu_d)
+        load_eps(1)
+        for g in range(3, GROUPS):
+            load_hd(g, False)
+            load_eps(g - 1)
+        load_eps(GROUPS - 1)
+
+        for i in R4:
+            trh(0, i, "B" + str(i))
+            cph("VS"[i % 2], 0, i)
+        qh(0)
+        for r in R4:
+            trw("wls", r, "A" + str(r))
+            cp_wls(r)
+        q_wls(0)
+        q_wls(1)
+        q_wls(2)
+        bias_t()
+        bias_half()
+        q_wls(3)
+        for j in R4:
+            ls(0, j)
+        for j in R4:
+            ex(0, j)
+        bias_c4()
+        hb = ("B2", "B3", "B0", "B1")
+        for i in R4:
+            trh(1, i, hb[i])
+            cph("VS"[i % 2], 1, i)
+        qh(1)
+        for j in R4:
+            etr(0, j)
+        for j in R4:
+            ph(0, j)
+            pc(0, j)
+        for i in R4:
+            trh(2, i, hb[i])
+        for i in R4:
+            cph("S", 2, i)
+        for j in R4:
+            ls(1, j)
+        qh(2)
+        for j in R4:
+            ex(1, j)
+        for r in R4:
+            pend["wmu", r] = transpose_tile(w_sb["wmu"], r, hb[r])
+            cp_wmu("VS"[r % 2], r)
+        for j in R4:
+            etr(1, j)
+        for j in R4:
+            ph(1, j)
+            pc(1, j)
+        qh("wmu")
+        for i in R4:
+            trh(3, i, hb[i])
+        for g in range(LAG, GROUPS):
+            if g + 1 < GROUPS:
+                for i in R4:
+                    cph("S", g + 1, i)
+            for j in R4:
+                ls(g, j)
+            if g + 1 < GROUPS:
+                qh(g + 1)
+            for j in R4:
+                ex(g, j)
+            for i in R4:
+                mu(g - LAG, i)
+            for i in R4:
+                rs(g - LAG, i)
+            store(g - LAG, 0, T4)
+            for j in R4:
+                etr(g, j)
+            for j in R4:
+                ph(g, j)
+                pc(g, j)
+            if g + 2 < GROUPS:
+                for i in R4:
+                    trh(g + 2, i, "B" + str(i))
+        for g in range(GROUPS - LAG, GROUPS):
+            for i in R4:
+                mu(g, i)
+            for i in R4:
+                rs(g, i)
+                store(g, i, i + 1)

@@ -38,6 +38,7 @@ def tile_vae_pb_t_kernel(tc, hd, W_mu_d, b_mu_d, W_ls_d, b_ls_d, eps_x, out):
         etp = ctx.enter_context(tc.tile_pool(name="etp", bufs=4))
         prodp = ctx.enter_context(tc.tile_pool(name="prodp", bufs=4))
         resp = ctx.enter_context(tc.tile_pool(name="resp", bufs=3))
+        permp = ctx.enter_context(tc.tile_pool(name="permp", bufs=2))
         psum = ctx.enter_context(tc.psum_pool(name="psum", bufs=1))
         ctx.enter_context(tc.manual_schedule())
 
@@ -65,6 +66,7 @@ def tile_vae_pb_t_kernel(tc, hd, W_mu_d, b_mu_d, W_ls_d, b_ls_d, eps_x, out):
         pend, grp, hq = {}, {}, {}
         wpend, wls_grp, wq = {}, {}, {}
         ls_ps, et_sb, e_ps, mu_ps, prod, res = {}, {}, {}, {}, {}, {}
+        sorted_sb = {}
         small = {}
 
         def load_hd(g, pieces):
@@ -95,6 +97,22 @@ def tile_vae_pb_t_kernel(tc, hd, W_mu_d, b_mu_d, W_ls_d, b_ls_d, eps_x, out):
                 nc.tensor.transpose(bk[:, s, :], words[:, c0 : (c0 // 256 + 1) * 256 : 2], ident[:])
             return bk
 
+        def sort_words(g, i):
+            if g not in sorted_sb:
+                sorted_sb[g] = permp.tile([P, T4 * K], BF16, tag="sorted", name="sorted")
+            tile_words = slice(i * 512, (i + 1) * 512)
+            src = hd_sb[g][:].bitcast(F32)[:, tile_words].rearrange("p (c q u) -> p c u q", c=PASSES, u=2)
+            dst = sorted_sb[g][:].bitcast(F32)[:, tile_words].rearrange("p (c u q) -> p c u q", c=PASSES, u=2)
+            nc.scalar.copy(out=dst, in_=src)
+
+        def transpose_sorted(g, i, tag):
+            words = sorted_sb[g][:].bitcast(F32)
+            bk = bank(tag, [P, 4, P])
+            for s in range(4):
+                c0 = i * 512 + s * P
+                nc.tensor.transpose(bk[:, s, :], words[:, c0 : c0 + P], ident[:])
+            return bk
+
         def copy_out(eng, dst, bk):
             src = bk[:].rearrange("p (g u) b -> p g b u", u=2)
             if eng == "V":
@@ -118,7 +136,10 @@ def tile_vae_pb_t_kernel(tc, hd, W_mu_d, b_mu_d, W_ls_d, b_ls_d, eps_x, out):
             return codes, scales
 
         def trh(g, i, tag):
-            pend[g, i] = transpose_tile(hd_sb[g], i, tag)
+            if g in sorted_sb:
+                pend[g, i] = transpose_sorted(g, i, tag)
+            else:
+                pend[g, i] = transpose_tile(hd_sb[g], i, tag)
 
         def cph(eng, g, i):
             if g not in grp:
@@ -277,6 +298,8 @@ def tile_vae_pb_t_kernel(tc, hd, W_mu_d, b_mu_d, W_ls_d, b_ls_d, eps_x, out):
         for r in R4:
             pend["wmu", r] = transpose_tile(w_sb["wmu"], r, hb[r])
             cp_wmu("VS"[r % 2], r)
+        for i in R4:
+            sort_words(3, i)
         for j in R4:
             etr(1, j)
         for j in R4:
@@ -295,6 +318,9 @@ def tile_vae_pb_t_kernel(tc, hd, W_mu_d, b_mu_d, W_ls_d, b_ls_d, eps_x, out):
                 qh(g + 1)
             for j in R4:
                 ex(g, j)
+            if g + 2 < GROUPS:
+                for i in R4:
+                    sort_words(g + 2, i)
             for i in R4:
                 mu(g - LAG, i)
             for i in R4:

@@ -103,7 +103,7 @@ def tile_vae_pb_t_kernel(tc, hd, W_mu_d, b_mu_d, W_ls_d, b_ls_d, eps_x, out):
             tile_words = slice(i * 512, (i + 1) * 512)
             src = hd_sb[g][:].bitcast(F32)[:, tile_words].rearrange("p (c q u) -> p c u q", c=PASSES, u=2)
             dst = sorted_sb[g][:].bitcast(F32)[:, tile_words].rearrange("p (c u q) -> p c u q", c=PASSES, u=2)
-            nc.scalar.copy(out=dst, in_=src)
+            nc.vector.tensor_copy(out=dst, in_=src)
 
         def transpose_sorted(g, i, tag):
             words = sorted_sb[g][:].bitcast(F32)
@@ -190,14 +190,13 @@ def tile_vae_pb_t_kernel(tc, hd, W_mu_d, b_mu_d, W_ls_d, b_ls_d, eps_x, out):
             nc.tensor.matmul(out=small["c"][:], lhsT=ones[:], rhs=brow_mu[:], start=True, stop=True)
 
         half_bls = const.tile([P, T4], F32, name="half_bls")
-        c4 = const.tile([P, T4 * XO], F32, name="c4")
+        c_mu = const.tile([P, XO], F32, name="c_mu")
 
         def bias_half():
             nc.vector.tensor_scalar_mul(out=half_bls[:], in0=small["bt"][:, 0:T4], scalar1=0.5)
 
-        def bias_c4():
-            for i in range(T4):
-                nc.vector.tensor_copy(out=c4[:, i * XO : (i + 1) * XO], in_=small["c"][:])
+        def bias_c():
+            nc.vector.tensor_copy(out=c_mu[:], in_=small["c"][:])
 
         def ls(g, j):
             ls_ps[g, j] = bank("A" + str(j), [P, 512])
@@ -228,7 +227,7 @@ def tile_vae_pb_t_kernel(tc, hd, W_mu_d, b_mu_d, W_ls_d, b_ls_d, eps_x, out):
         def pc(g, j):
             cols = slice(j * P, (j + 1) * P)
             nc.gpsimd.tensor_tensor(
-                out=by_tile(prod[g])[:, :, cols], in0=by_tile(prod[g])[:, :, cols], in1=by_tile(c4)[:, :, cols], op=ALU.add
+                out=by_tile(prod[g])[:, :, cols], in0=by_tile(prod[g])[:, :, cols], in1=c_mu[:, cols].unsqueeze(1).to_broadcast([P, T4, P]), op=ALU.add
             )
 
         def mu(g, i):
@@ -249,8 +248,8 @@ def tile_vae_pb_t_kernel(tc, hd, W_mu_d, b_mu_d, W_ls_d, b_ls_d, eps_x, out):
         load_hd(0, True)
         load_w("wls", W_ls_d)
         load_hd(1, True)
-        load_eps(0)
         load_hd(2, False)
+        load_eps(0)
         load_w("wmu", W_mu_d)
         load_eps(1)
         for g in range(3, GROUPS):
@@ -275,7 +274,7 @@ def tile_vae_pb_t_kernel(tc, hd, W_mu_d, b_mu_d, W_ls_d, b_ls_d, eps_x, out):
             ls(0, j)
         for j in R4:
             ex(0, j)
-        bias_c4()
+        bias_c()
         hb = ("B2", "B3", "B0", "B1")
         for i in R4:
             trh(1, i, hb[i])
@@ -298,8 +297,6 @@ def tile_vae_pb_t_kernel(tc, hd, W_mu_d, b_mu_d, W_ls_d, b_ls_d, eps_x, out):
         for r in R4:
             pend["wmu", r] = transpose_tile(w_sb["wmu"], r, hb[r])
             cp_wmu("VS"[r % 2], r)
-        for i in R4:
-            sort_words(3, i)
         for j in R4:
             etr(1, j)
         for j in R4:

@@ -17,6 +17,7 @@ T4 = 4
 GROUPS = B // (P * T4)
 K_PASS = 512
 PASSES = K // K_PASS
+SORTED_TILES = (1, 2, 3)
 LAG = 2
 FLOPS = 2 * B * K * 2 * XO
 
@@ -103,7 +104,7 @@ def tile_vae_pb_t_kernel(tc, hd, W_mu_d, b_mu_d, W_ls_d, b_ls_d, eps_x, out):
             tile_words = slice(i * 512, (i + 1) * 512)
             src = hd_sb[g][:].bitcast(F32)[:, tile_words].rearrange("p (c q u) -> p c u q", c=PASSES, u=2)
             dst = sorted_sb[g][:].bitcast(F32)[:, tile_words].rearrange("p (c u q) -> p c u q", c=PASSES, u=2)
-            nc.vector.tensor_copy(out=dst, in_=src)
+            nc.scalar.copy(out=dst, in_=src)
 
         def transpose_sorted(g, i, tag):
             words = sorted_sb[g][:].bitcast(F32)
@@ -136,7 +137,7 @@ def tile_vae_pb_t_kernel(tc, hd, W_mu_d, b_mu_d, W_ls_d, b_ls_d, eps_x, out):
             return codes, scales
 
         def trh(g, i, tag):
-            if g in sorted_sb:
+            if g in sorted_sb and i in SORTED_TILES:
                 pend[g, i] = transpose_sorted(g, i, tag)
             else:
                 pend[g, i] = transpose_tile(hd_sb[g], i, tag)
@@ -226,7 +227,8 @@ def tile_vae_pb_t_kernel(tc, hd, W_mu_d, b_mu_d, W_ls_d, b_ls_d, eps_x, out):
 
         def pc(g, j):
             cols = slice(j * P, (j + 1) * P)
-            nc.gpsimd.tensor_tensor(
+            eng = nc.vector if (g, j) == (GROUPS - 1, T4 - 1) else nc.gpsimd
+            eng.tensor_tensor(
                 out=by_tile(prod[g])[:, :, cols], in0=by_tile(prod[g])[:, :, cols], in1=c_mu[:, cols].unsqueeze(1).to_broadcast([P, T4, P]), op=ALU.add
             )
 
@@ -316,7 +318,7 @@ def tile_vae_pb_t_kernel(tc, hd, W_mu_d, b_mu_d, W_ls_d, b_ls_d, eps_x, out):
             for j in R4:
                 ex(g, j)
             if g + 2 < GROUPS:
-                for i in R4:
+                for i in SORTED_TILES:
                     sort_words(g + 2, i)
             for i in R4:
                 mu(g - LAG, i)
@@ -327,13 +329,16 @@ def tile_vae_pb_t_kernel(tc, hd, W_mu_d, b_mu_d, W_ls_d, b_ls_d, eps_x, out):
                 etr(g, j)
             for j in R4:
                 ph(g, j)
-                pc(g, j)
+                if (g, j) != (GROUPS - 1, T4 - 1):
+                    pc(g, j)
             if g + 2 < GROUPS:
                 for i in R4:
                     trh(g + 2, i, "B" + str(i))
         for g in range(GROUPS - LAG, GROUPS):
             for i in R4:
                 mu(g, i)
+            if g == GROUPS - 1:
+                pc(g, T4 - 1)
             for i in R4:
                 rs(g, i)
                 store(g, i, i + 1)

@@ -17,7 +17,6 @@ T4 = 4
 GROUPS = B // (P * T4)
 K_PASS = 512
 PASSES = K // K_PASS
-SORTED_TILES = (1, 2, 3)
 LAG = 2
 FLOPS = 2 * B * K * 2 * XO
 
@@ -67,7 +66,7 @@ def tile_vae_pb_t_kernel(tc, hd, W_mu_d, b_mu_d, W_ls_d, b_ls_d, eps_x, out):
         pend, grp, hq = {}, {}, {}
         wpend, wls_grp, wq = {}, {}, {}
         ls_ps, et_sb, e_ps, mu_ps, prod, res = {}, {}, {}, {}, {}, {}
-        sorted_sb = {}
+        sorted_sb, sorted_tiles = {}, []
         small = {}
 
         def load_hd(g, pieces):
@@ -98,13 +97,21 @@ def tile_vae_pb_t_kernel(tc, hd, W_mu_d, b_mu_d, W_ls_d, b_ls_d, eps_x, out):
                 nc.tensor.transpose(bk[:, s, :], words[:, c0 : (c0 // 256 + 1) * 256 : 2], ident[:])
             return bk
 
-        def sort_words(g, i):
+        def sort_words(eng, g, i):
             if g not in sorted_sb:
                 sorted_sb[g] = permp.tile([P, T4 * K], BF16, tag="sorted", name="sorted")
+            sorted_tiles.append((g, i))
             tile_words = slice(i * 512, (i + 1) * 512)
-            src = hd_sb[g][:].bitcast(F32)[:, tile_words].rearrange("p (c q u) -> p c u q", c=PASSES, u=2)
-            dst = sorted_sb[g][:].bitcast(F32)[:, tile_words].rearrange("p (c u q) -> p c u q", c=PASSES, u=2)
-            nc.scalar.copy(out=dst, in_=src)
+            src = hd_sb[g][:].bitcast(F32)[:, tile_words].rearrange(
+                "p (c b q u) -> p c b u q", c=PASSES, q=4, u=2
+            )
+            dst = sorted_sb[g][:].bitcast(F32)[:, tile_words].rearrange(
+                "p (c u b q) -> p c b u q", c=PASSES, q=4, u=2
+            )
+            if eng == "V":
+                nc.vector.tensor_copy(out=dst, in_=src)
+            else:
+                nc.scalar.copy(out=dst, in_=src)
 
         def transpose_sorted(g, i, tag):
             words = sorted_sb[g][:].bitcast(F32)
@@ -125,19 +132,13 @@ def tile_vae_pb_t_kernel(tc, hd, W_mu_d, b_mu_d, W_ls_d, b_ls_d, eps_x, out):
             gw = t[:].bitcast(F32).rearrange("p (g c u) -> p g c u", g=PASSES, u=2)
             return gw[:, :, i * P : (i + 1) * P, :]
 
-        def quantise_group(t, pool, tag):
+        def new_codes(pool, tag):
             codes = pool.tile([P, PASSES * 512], U32, tag=tag + "c", name=tag + "c", align_bytes=64)
             scales = pool.tile([P, PASSES * 512], U8, tag=tag + "s", name=tag + "s", align_bytes=64)
-            for c in range(PASSES):
-                nc.vector.quantize_mx(
-                    out=codes[:, c * 512 : (c + 1) * 512].bitcast(FP8X4),
-                    scales=scales[:, c * 512 : (c + 1) * 512],
-                    in_=t[:, c * 2048 : (c + 1) * 2048],
-                )
             return codes, scales
 
         def trh(g, i, tag):
-            if g in sorted_sb and i in SORTED_TILES:
+            if (g, i) in sorted_tiles:
                 pend[g, i] = transpose_sorted(g, i, tag)
             else:
                 pend[g, i] = transpose_tile(hd_sb[g], i, tag)
@@ -147,11 +148,19 @@ def tile_vae_pb_t_kernel(tc, hd, W_mu_d, b_mu_d, W_ls_d, b_ls_d, eps_x, out):
                 grp[g] = grpp.tile([P, T4 * K], BF16, tag="grp", name="grp", align_bytes=64)
             copy_out(eng, group_slot(grp[g], i), pend[g, i])
 
+        def qh_pass(g, c):
+            if g not in hq:
+                hq[g] = new_codes(const, "wmu") if g == "wmu" else new_codes(hcp, "h")
+            codes, scales = hq[g]
+            nc.vector.quantize_mx(
+                out=codes[:, c * 512 : (c + 1) * 512].bitcast(FP8X4),
+                scales=scales[:, c * 512 : (c + 1) * 512],
+                in_=grp[g][:, c * 2048 : (c + 1) * 2048],
+            )
+
         def qh(g):
-            if g == "wmu":
-                hq[g] = quantise_group(grp[g], const, "wmu")
-            else:
-                hq[g] = quantise_group(grp[g], hcp, "h")
+            for c in range(PASSES):
+                qh_pass(g, c)
 
         def trw(nm, r, tag):
             wpend[nm, r] = transpose_tile(w_sb[nm], r, tag)
@@ -236,14 +245,16 @@ def tile_vae_pb_t_kernel(tc, hd, W_mu_d, b_mu_d, W_ls_d, b_ls_d, eps_x, out):
             mu_ps[g, i] = bank("B" + str(i), [P, XO])
             mx(mu_ps[g, i][:], hq[g], 512, i * P, hq["wmu"], 512)
 
-        def rs(g, i):
+        def rs(g, i, n0=0, n1=XO):
             if g not in res:
                 res[g] = resp.tile([P, T4 * XO], F32, tag="res", name="res")
-            cols = slice(i * XO, (i + 1) * XO)
-            nc.vector.tensor_tensor(out=res[g][:, cols], in0=mu_ps[g, i][:], in1=prod[g][:, cols], op=ALU.add)
+            cols = slice(i * XO + n0, i * XO + n1)
+            nc.vector.tensor_tensor(
+                out=res[g][:, cols], in0=mu_ps[g, i][:, n0:n1], in1=prod[g][:, cols], op=ALU.add
+            )
 
-        def store(g, i0, i1):
-            cols = slice(i0 * XO, i1 * XO)
+        def store(g, i0, i1, n0=0, n1=XO):
+            cols = slice(i0 * XO + n0, (i1 - 1) * XO + n1)
             nc.sync.dma_start(out=out_v[g][:, cols], in_=res[g][:, cols])
 
         R4 = range(T4)
@@ -262,11 +273,12 @@ def tile_vae_pb_t_kernel(tc, hd, W_mu_d, b_mu_d, W_ls_d, b_ls_d, eps_x, out):
         for i in R4:
             trh(0, i, "B" + str(i))
             cph("VS"[i % 2], 0, i)
-        qh(0)
+        qh_pass(0, 0)
         for r in R4:
             trw("wls", r, "A" + str(r))
             cp_wls(r)
         q_wls(0)
+        qh_pass(0, 1)
         q_wls(1)
         q_wls(2)
         bias_t()
@@ -277,6 +289,8 @@ def tile_vae_pb_t_kernel(tc, hd, W_mu_d, b_mu_d, W_ls_d, b_ls_d, eps_x, out):
         for j in R4:
             ex(0, j)
         bias_c()
+        for i in R4:
+            sort_words("V", 1, i)
         hb = ("B2", "B3", "B0", "B1")
         for i in R4:
             trh(1, i, hb[i])
@@ -299,6 +313,8 @@ def tile_vae_pb_t_kernel(tc, hd, W_mu_d, b_mu_d, W_ls_d, b_ls_d, eps_x, out):
         for r in R4:
             pend["wmu", r] = transpose_tile(w_sb["wmu"], r, hb[r])
             cp_wmu("VS"[r % 2], r)
+        for i in (2, 3):
+            sort_words("S", 3, i)
         for j in R4:
             etr(1, j)
         for j in R4:
@@ -310,7 +326,7 @@ def tile_vae_pb_t_kernel(tc, hd, W_mu_d, b_mu_d, W_ls_d, b_ls_d, eps_x, out):
         for g in range(LAG, GROUPS):
             if g + 1 < GROUPS:
                 for i in R4:
-                    cph("S", g + 1, i)
+                    cph("SSSV"[i], g + 1, i)
             for j in R4:
                 ls(g, j)
             if g + 1 < GROUPS:
@@ -318,8 +334,8 @@ def tile_vae_pb_t_kernel(tc, hd, W_mu_d, b_mu_d, W_ls_d, b_ls_d, eps_x, out):
             for j in R4:
                 ex(g, j)
             if g + 2 < GROUPS:
-                for i in SORTED_TILES:
-                    sort_words(g + 2, i)
+                for i in R4:
+                    sort_words("S", g + 2, i)
             for i in R4:
                 mu(g - LAG, i)
             for i in R4:
@@ -340,5 +356,7 @@ def tile_vae_pb_t_kernel(tc, hd, W_mu_d, b_mu_d, W_ls_d, b_ls_d, eps_x, out):
             if g == GROUPS - 1:
                 pc(g, T4 - 1)
             for i in R4:
-                rs(g, i)
-                store(g, i, i + 1)
+                step = XO // 2 if (g, i) == (GROUPS - 1, T4 - 1) else XO
+                for n in range(0, XO, step):
+                    rs(g, i, n, n + step)
+                    store(g, i, i + 1, n, n + step)

from contextlib import ExitStack

import concourse.mybir as mybir
from concourse.masks import make_identity

F32 = mybir.dt.float32
BF16 = mybir.dt.bfloat16
U32 = mybir.dt.uint32
U8 = mybir.dt.uint8
FP8X4 = mybir.dt.float8_e4m3fn_x4
ACT = mybir.ActivationFunctionType
ALU = mybir.AluOpType

P = 128
B, K, XO = 4096, 1024, 512
T4 = 4
GROUPS = B // (P * T4)
K_PASS = 512
PASSES = K // K_PASS
LAG = 2
FLOPS = 2 * B * K * 2 * XO


def tile_vae_pb_t_kernel(tc, hd, W_mu_d, b_mu_d, W_ls_d, b_ls_d, eps_x, out):
    nc = tc.nc
    hd_v = hd.rearrange("(g p i) k -> g p (i k)", p=P, i=T4)
    hd_pieces = hd.rearrange("(g p i) k -> g i p k", p=P, i=T4)
    eps_v = eps_x.rearrange("(g p i) n -> g p (i n)", p=P, i=T4)
    out_v = out.rearrange("(g p i) n -> g p (i n)", p=P, i=T4)

    with ExitStack() as ctx:
        const = ctx.enter_context(tc.tile_pool(name="const", bufs=1))
        raw = ctx.enter_context(tc.tile_pool(name="raw", bufs=4))
        epsp = ctx.enter_context(tc.tile_pool(name="epsp", bufs=GROUPS))
        grpp = ctx.enter_context(tc.tile_pool(name="grpp", bufs=2))
        grpw = ctx.enter_context(tc.tile_pool(name="grpw", bufs=4))
        hcp = ctx.enter_context(tc.tile_pool(name="hcp", bufs=5))
        etp = ctx.enter_context(tc.tile_pool(name="etp", bufs=4))
        prodp = ctx.enter_context(tc.tile_pool(name="prodp", bufs=4))
        resp = ctx.enter_context(tc.tile_pool(name="resp", bufs=3))
        permp = ctx.enter_context(tc.tile_pool(name="permp", bufs=2))
        psum = ctx.enter_context(tc.psum_pool(name="psum", bufs=1))
        ctx.enter_context(tc.manual_schedule())

        def bank(tag, shape, dtype=F32):
            return psum.tile(shape, dtype, tag=tag, name="ps" + tag)

        ident = const.tile([P, P], F32, name="ident")
        make_identity(nc, ident[:])
        ident_bf = const.tile([P, P], BF16, name="ident_bf")
        make_identity(nc, ident_bf[:])
        brow_mu = const.tile([P, XO], BF16, name="brow_mu")
        nc.vector.memset(brow_mu[:], 0.0)
        bcol = const.tile([P, P], BF16, name="bcol")
        nc.vector.memset(bcol[:], 0.0)
        ones = const.tile([P, P], BF16, name="ones")
        nc.vector.memset(ones[:], 1.0)
        warm = const.tile([P, 1], F32, name="warm")
        nc.vector.memset(warm[:], 0.0)
        nc.scalar.dma_start(out=bcol[0:T4, :], in_=b_ls_d.rearrange("(j q) -> j q", q=P))
        nc.scalar.dma_start(out=brow_mu[0:1, :], in_=b_mu_d.rearrange("(o n) -> o n", o=1))
        warm2 = const.tile([P, 1], F32, name="warm2")
        nc.scalar.activation(out=warm2[:], in_=warm[:], func=ACT.Exp)

        hd_sb, eps_sb, w_sb = {}, {}, {}
        pend, grp, hq = {}, {}, {}
        wpend, wls_grp, wq = {}, {}, {}
        ls_ps, et_sb, e_ps, mu_ps, prod, res = {}, {}, {}, {}, {}, {}
        sorted_sb, sorted_tiles = {}, []
        small = {}

        def load_hd(g, pieces):
            t = raw.tile([P, T4 * K], BF16, tag="raw", name="hd_sb")
            if pieces:
                for i in range(T4):
                    nc.sync.dma_start(out=t[:, i * K : (i + 1) * K], in_=hd_pieces[g, i])
            else:
                nc.sync.dma_start(out=t[:], in_=hd_v[g])
            hd_sb[g] = t

        def load_w(nm, w):
            t = const.tile([P, T4 * K], BF16, name=nm)
            for r in range(T4):
                nc.sync.dma_start(out=t[:, r * K : (r + 1) * K], in_=w[r * P : (r + 1) * P, :])
            w_sb[nm] = t

        def load_eps(g):
            t = epsp.tile([P, T4 * XO], BF16, tag="eps", name="eps_sb")
            nc.sync.dma_start(out=t[:], in_=eps_v[g])
            eps_sb[g] = t

        def transpose_tile(src, i, tag):
            words = src[:].bitcast(F32)
            bk = bank(tag, [P, 4, P])
            for s in range(4):
                c0 = i * 512 + (s // 2) * 256 + s % 2
                nc.tensor.transpose(bk[:, s, :], words[:, c0 : (c0 // 256 + 1) * 256 : 2], ident[:])
            return bk

        def sort_words(eng, g, i):
            if g not in sorted_sb:
                sorted_sb[g] = permp.tile([P, T4 * K], BF16, tag="sorted", name="sorted")
            sorted_tiles.append((g, i))
            tile_words = slice(i * 512, (i + 1) * 512)
            src = hd_sb[g][:].bitcast(F32)[:, tile_words].rearrange(
                "p (c b q u) -> p c b u q", c=PASSES, q=4, u=2
            )
            dst = sorted_sb[g][:].bitcast(F32)[:, tile_words].rearrange(
                "p (c u b q) -> p c b u q", c=PASSES, q=4, u=2
            )
            if eng == "V":
                nc.vector.tensor_copy(out=dst, in_=src)
            else:
                nc.scalar.copy(out=dst, in_=src)

        def transpose_sorted(g, i, tag):
            words = sorted_sb[g][:].bitcast(F32)
            bk = bank(tag, [P, 4, P])
            for s in range(4):
                c0 = i * 512 + s * P
                nc.tensor.transpose(bk[:, s, :], words[:, c0 : c0 + P], ident[:])
            return bk

        def copy_out(eng, dst, bk):
            src = bk[:].rearrange("p (g u) b -> p g b u", u=2)
            if eng == "V":
                nc.vector.tensor_copy(out=dst, in_=src)
            else:
                nc.scalar.copy(out=dst, in_=src)

        def group_slot(t, i):
            gw = t[:].bitcast(F32).rearrange("p (g c u) -> p g c u", g=PASSES, u=2)
            return gw[:, :, i * P : (i + 1) * P, :]

        def new_codes(pool, tag):
            codes = pool.tile([P, PASSES * 512], U32, tag=tag + "c", name=tag + "c", align_bytes=64)
            scales = pool.tile([P, PASSES * 512], U8, tag=tag + "s", name=tag + "s", align_bytes=64)
            return codes, scales

        def trh(g, i, tag):
            if (g, i) in sorted_tiles:
                pend[g, i] = transpose_sorted(g, i, tag)
            else:
                pend[g, i] = transpose_tile(hd_sb[g], i, tag)

        def cph(eng, g, i):
            if g not in grp:
                grp[g] = grpp.tile([P, T4 * K], BF16, tag="grp", name="grp", align_bytes=64)
            copy_out(eng, group_slot(grp[g], i), pend[g, i])

        def qh_pass(g, c):
            if g not in hq:
                hq[g] = new_codes(const, "wmu") if g == "wmu" else new_codes(hcp, "h")
            codes, scales = hq[g]
            nc.vector.quantize_mx(
                out=codes[:, c * 512 : (c + 1) * 512].bitcast(FP8X4),
                scales=scales[:, c * 512 : (c + 1) * 512],
                in_=grp[g][:, c * 2048 : (c + 1) * 2048],
            )

        def qh(g):
            for c in range(PASSES):
                qh_pass(g, c)

        def trw(nm, r, tag):
            wpend[nm, r] = transpose_tile(w_sb[nm], r, tag)

        def cp_wls(r):
            t = grpw.tile([P, K], BF16, tag="grpw", name="grpw", align_bytes=64)
            copy_out("S", t[:].bitcast(F32).rearrange("p (g c u) -> p g c u", g=PASSES, u=2), wpend["wls", r])
            wls_grp[r] = t

        def q_wls(r):
            codes = const.tile([P, PASSES * P], U32, name="wlsc" + str(r), align_bytes=64)
            scales = const.tile([P, PASSES * P], U8, name="wlss" + str(r), align_bytes=64)
            nc.vector.quantize_mx(out=codes[:].bitcast(FP8X4), scales=scales[:], in_=wls_grp[r][:])
            wq[r] = (codes, scales)

        def cp_wmu(eng, r):
            cph(eng, "wmu", r)

        def mx(acc, stat, s_pitch, s0, mov, m_pitch):
            for c in range(PASSES):
                a = c * s_pitch + s0
                b = c * m_pitch
                nc.tensor.matmul_mx(
                    out=acc,
                    lhsT=stat[0][:, a : a + P].bitcast(FP8X4),
                    lhsT_scale=stat[1][:, a : a + P],
                    rhs=mov[0][:, b : b + 512].bitcast(FP8X4),
                    rhs_scale=mov[1][:, b : b + 512],
                    start=(c == 0),
                    stop=(c == PASSES - 1),
                )

        def bias_t():
            small["bt"] = bank("B0", [P, P], BF16)
            nc.tensor.transpose(small["bt"][:], bcol[:], ident_bf[:])
            small["c"] = bank("B1", [P, XO])
            nc.tensor.matmul(out=small["c"][:], lhsT=ones[:], rhs=brow_mu[:], start=True, stop=True)

        half_bls = const.tile([P, T4], F32, name="half_bls")
        c_mu = const.tile([P, XO], F32, name="c_mu")

        def bias_half():
            nc.vector.tensor_scalar_mul(out=half_bls[:], in0=small["bt"][:, 0:T4], scalar1=0.5)

        def bias_c():
            nc.vector.tensor_copy(out=c_mu[:], in_=small["c"][:])

        def ls(g, j):
            ls_ps[g, j] = bank("A" + str(j), [P, 512])
            mx(ls_ps[g, j][:], wq[j], P, 0, hq[g], 512)

        def ex(g, j):
            et_sb[g, j] = etp.tile([P, 512], F32, tag="et", name="et")
            nc.scalar.activation(
                out=et_sb[g, j][:], in_=ls_ps[g, j][:], func=ACT.Exp, bias=half_bls[:, j : j + 1], scale=0.5
            )

        def etr(g, j):
            e_ps[g, j] = bank("A" + str(j), [P, T4, P])
            for i in range(T4):
                nc.tensor.transpose(e_ps[g, j][:, i, :], et_sb[g, j][:, i * P : (i + 1) * P], ident[:])

        def by_tile(t):
            return t[:].rearrange("p (i n) -> p i n", i=T4)

        def ph(g, j):
            if g not in prod:
                prod[g] = prodp.tile([P, T4 * XO], F32, tag="prod", name="prod")
            cols = slice(j * P, (j + 1) * P)
            nc.vector.tensor_tensor(
                out=by_tile(prod[g])[:, :, cols], in0=e_ps[g, j][:], in1=by_tile(eps_sb[g])[:, :, cols], op=ALU.mult
            )

        def pc(g, j):
            cols = slice(j * P, (j + 1) * P)
            eng = nc.vector if (g, j) == (GROUPS - 1, T4 - 1) else nc.gpsimd
            eng.tensor_tensor(
                out=by_tile(prod[g])[:, :, cols], in0=by_tile(prod[g])[:, :, cols], in1=c_mu[:, cols].unsqueeze(1).to_broadcast([P, T4, P]), op=ALU.add
            )

        def mu(g, i):
            mu_ps[g, i] = bank("B" + str(i), [P, XO])
            mx(mu_ps[g, i][:], hq[g], 512, i * P, hq["wmu"], 512)

        def rs(g, i, n0=0, n1=XO):
            if g not in res:
                res[g] = resp.tile([P, T4 * XO], F32, tag="res", name="res")
            cols = slice(i * XO + n0, i * XO + n1)
            nc.vector.tensor_tensor(
                out=res[g][:, cols], in0=mu_ps[g, i][:, n0:n1], in1=prod[g][:, cols], op=ALU.add
            )

        def store(g, i0, i1, n0=0, n1=XO):
            cols = slice(i0 * XO + n0, (i1 - 1) * XO + n1)
            nc.sync.dma_start(out=out_v[g][:, cols], in_=res[g][:, cols])

        R4 = range(T4)
        load_hd(0, True)
        load_w("wls", W_ls_d)
        load_hd(1, True)
        load_hd(2, False)
        load_eps(0)
        load_w("wmu", W_mu_d)
        load_eps(1)
        for g in range(3, GROUPS):
            load_hd(g, False)
            load_eps(g - 1)
        load_eps(GROUPS - 1)

        for i in R4:
            trh(0, i, "B" + str(i))
            cph("VS"[i % 2], 0, i)
        qh_pass(0, 0)
        for r in R4:
            trw("wls", r, "A" + str(r))
            cp_wls(r)
        q_wls(0)
        qh_pass(0, 1)
        q_wls(1)
        q_wls(2)
        bias_t()
        bias_half()
        q_wls(3)
        for j in R4:
            ls(0, j)
        for j in R4:
            ex(0, j)
        bias_c()
        for i in R4:
            sort_words("V", 1, i)
        hb = ("B2", "B3", "B0", "B1")
        for i in R4:
            trh(1, i, hb[i])
            cph("VS"[i % 2], 1, i)
        qh(1)
        for j in R4:
            etr(0, j)
        for j in R4:
            ph(0, j)
            pc(0, j)
        for i in R4:
            trh(2, i, hb[i])
        for i in R4:
            cph("S", 2, i)
        for j in R4:
            ls(1, j)
        qh(2)
        for j in R4:
            ex(1, j)
        for r in R4:
            pend["wmu", r] = transpose_tile(w_sb["wmu"], r, hb[r])
            cp_wmu("VS"[r % 2], r)
        for i in (2, 3):
            sort_words("S", 3, i)
        for j in R4:
            etr(1, j)
        for j in R4:
            ph(1, j)
            pc(1, j)
        qh("wmu")
        for i in R4:
            trh(3, i, hb[i])
        for g in range(LAG, GROUPS):
            if g + 1 < GROUPS:
                for i in R4:
                    cph("SSSV"[i], g + 1, i)
            for j in R4:
                ls(g, j)
            if g + 1 < GROUPS:
                qh(g + 1)
            for j in R4:
                ex(g, j)
            if g + 2 < GROUPS:
                for i in R4:
                    sort_words("S", g + 2, i)
            for i in R4:
                mu(g - LAG, i)
            for i in R4:
                rs(g - LAG, i)
            store(g - LAG, 0, T4)
            for j in R4:
                etr(g, j)
            for j in R4:
                ph(g, j)
                if (g, j) != (GROUPS - 1, T4 - 1):
                    pc(g, j)
            if g + 2 < GROUPS:
                for i in R4:
                    trh(g + 2, i, "B" + str(i))
        for g in range(GROUPS - LAG, GROUPS):
            for i in R4:
                mu(g, i)
            if g == GROUPS - 1:
                pc(g, T4 - 1)
            for i in R4:
                step = XO // 2 if (g, i) == (GROUPS - 1, T4 - 1) else XO
                for n in range(0, XO, step):
                    rs(g, i, n, n + step)
                    store(g, i, i + 1, n, n + step)
